import numpy as np
import ml_dtypes

BF16 = ml_dtypes.bfloat16


def bf(x):
    return np.asarray(x, np.float32).astype(BF16)


def f32(x):
    return np.asarray(x, np.float32)


def f64(x):
    return np.asarray(x).astype(np.float64)


def striped(idx):
    return np.tile(idx.reshape(-1, 16).T, (8, 1))


S, D, R, M, D2, N = 256, 128, 128, 128, 256, 128


def silu(v):
    return v / (1.0 + np.exp(-v))


def setup_inputs():
    q = np.sqrt(3.0)
    return {
        "table": bf(np.random.uniform(-q, q, (D, S))),
        "w_src": bf(np.random.standard_normal((D, M)) / np.sqrt(D + D2)),
        "h_dst": bf(np.random.uniform(-q, q, (D, N))),
        "rbf": bf(np.random.standard_normal((R, N))),
        "w_rbf": bf(np.random.standard_normal((R, D)) / np.sqrt(R)),
        "b_rbf": f32(0.1 * np.random.standard_normal((D, 1))),
        "w_rest": bf(np.random.standard_normal((D2, M)) / np.sqrt(D + D2)),
        "b_dense": f32(0.1 * np.random.standard_normal((M, 1))),
        "offs": striped(np.random.permutation(np.tile(np.arange(S), 2))[:N]),
    }


def reference(table, w_src, h_dst, rbf, w_rbf, b_rbf, w_rest, b_dense, offs):
    idx = offs[:16].T.reshape(-1)
    p = silu(f64(w_rbf).T @ f64(rbf) + f64(b_rbf))
    acc = f64(w_src).T @ f64(table)[:, idx]
    acc = acc + f64(w_rest).T @ np.concatenate([f64(h_dst), p], axis=0)
    return silu(acc + f64(b_dense))

@@ -1,0 +1,57 @@
+import concourse.mybir as mybir
+
+P = 128
+ATOMS = 256
+EDGES = 128
+FLOPS = 2 * 4 * P * P * EDGES
+
+BF16, F32, U16 = mybir.dt.bfloat16, mybir.dt.float32, mybir.dt.uint16
+SILU = mybir.ActivationFunctionType.Silu
+
+
+def tile_embeddinglayer_kernel(
+    tc, table, w_src, h_dst, rbf, w_rbf, b_rbf, w_rest, b_dense, offs, out
+):
+    nc = tc.nc
+    with (
+        tc.tile_pool(name="held", bufs=1) as held,
+        tc.psum_pool(name="psum", bufs=1) as psum,
+    ):
+        rbf_sb = held.tile([P, EDGES], BF16, name="rbf_sb")
+        nc.sync.dma_start(rbf_sb[:], rbf)
+        w_rbf_sb = held.tile([P, P], BF16, name="w_rbf_sb")
+        nc.scalar.dma_start(w_rbf_sb[:], w_rbf)
+        b_rbf_sb = held.tile([P, 1], F32, name="b_rbf_sb")
+        nc.gpsimd.dma_start(b_rbf_sb[:], b_rbf)
+
+        offsets = held.tile([P, EDGES // 16], U16, name="offsets")
+        nc.sync.dma_start(offsets[:], offs)
+        table_sb = held.tile([P, ATOMS], BF16, name="table_sb")
+        nc.sync.dma_start(table_sb[:], table)
+        w_src_sb = held.tile([P, P], BF16, name="w_src_sb")
+        nc.scalar.dma_start(w_src_sb[:], w_src)
+
+        h_dst_sb = held.tile([P, EDGES], BF16, name="h_dst_sb")
+        nc.sync.dma_start(h_dst_sb[:], h_dst)
+        w_dst_sb = held.tile([P, P], BF16, name="w_dst_sb")
+        nc.scalar.dma_start(w_dst_sb[:], w_rest[0:P, :])
+        w_p_sb = held.tile([P, P], BF16, name="w_p_sb")
+        nc.scalar.dma_start(w_p_sb[:], w_rest[P : 2 * P, :])
+        b_dense_sb = held.tile([P, 1], F32, name="b_dense_sb")
+        nc.gpsimd.dma_start(b_dense_sb[:], b_dense)
+
+        proj = psum.tile([P, EDGES], F32, name="proj")
+        nc.tensor.matmul(proj[:], w_rbf_sb[:], rbf_sb[:], start=True, stop=True)
+        p_sb = held.tile([P, EDGES], BF16, name="p_sb")
+        nc.scalar.activation(p_sb[:], proj[:], SILU, bias=b_rbf_sb[:])
+
+        acc = psum.tile([P, EDGES], F32, name="acc")
+        nc.tensor.matmul(
+            acc[:], w_src_sb[:], table_sb[:].indirect(offsets[:]), start=True, stop=False
+        )
+        nc.tensor.matmul(acc[:], w_dst_sb[:], h_dst_sb[:], start=False, stop=False)
+        nc.tensor.matmul(acc[:], w_p_sb[:], p_sb[:], start=False, stop=True)
+
+        out_sb = held.tile([P, EDGES], F32, name="out_sb")
+        nc.scalar.activation(out_sb[:], acc[:], SILU, bias=b_dense_sb[:])
+        nc.sync.dma_start(out, out_sb[:])

@@ -22,7 +22,7 @@ def tile_embeddinglayer_kernel(
         w_rbf_sb = held.tile([P, P], BF16, name="w_rbf_sb")
         nc.scalar.dma_start(w_rbf_sb[:], w_rbf)
         b_rbf_sb = held.tile([P, 1], F32, name="b_rbf_sb")
-        nc.gpsimd.dma_start(b_rbf_sb[:], b_rbf)
+        nc.sync.dma_start(b_rbf_sb[:], b_rbf)
 
         offsets = held.tile([P, EDGES // 16], U16, name="offsets")
         nc.sync.dma_start(offsets[:], offs)
@@ -38,7 +38,11 @@ def tile_embeddinglayer_kernel(
         w_p_sb = held.tile([P, P], BF16, name="w_p_sb")
         nc.scalar.dma_start(w_p_sb[:], w_rest[P : 2 * P, :])
         b_dense_sb = held.tile([P, 1], F32, name="b_dense_sb")
-        nc.gpsimd.dma_start(b_dense_sb[:], b_dense)
+        nc.scalar.dma_start(b_dense_sb[:], b_dense)
+
+        warm = held.tile([P, 1], F32, name="warm")
+        nc.vector.memset(warm[:], 0.0)
+        nc.scalar.activation(warm[:], warm[:], SILU)
 
         proj = psum.tile([P, EDGES], F32, name="proj")
         nc.tensor.matmul(proj[:], w_rbf_sb[:], rbf_sb[:], start=True, stop=True)

@@ -22,7 +22,7 @@ def tile_embeddinglayer_kernel(
         w_rbf_sb = held.tile([P, P], BF16, name="w_rbf_sb")
         nc.scalar.dma_start(w_rbf_sb[:], w_rbf)
         b_rbf_sb = held.tile([P, 1], F32, name="b_rbf_sb")
-        nc.sync.dma_start(b_rbf_sb[:], b_rbf)
+        nc.gpsimd.dma_start(b_rbf_sb[:], b_rbf)
 
         offsets = held.tile([P, EDGES // 16], U16, name="offsets")
         nc.sync.dma_start(offsets[:], offs)
@@ -38,7 +38,7 @@ def tile_embeddinglayer_kernel(
         w_p_sb = held.tile([P, P], BF16, name="w_p_sb")
         nc.scalar.dma_start(w_p_sb[:], w_rest[P : 2 * P, :])
         b_dense_sb = held.tile([P, 1], F32, name="b_dense_sb")
-        nc.scalar.dma_start(b_dense_sb[:], b_dense)
+        nc.gpsimd.dma_start(b_dense_sb[:], b_dense)
 
         warm = held.tile([P, 1], F32, name="warm")
         nc.vector.memset(warm[:], 0.0)

@@ -18,11 +18,11 @@ def tile_embeddinglayer_kernel(
         tc.psum_pool(name="psum", bufs=1) as psum,
     ):
         rbf_sb = held.tile([P, EDGES], BF16, name="rbf_sb")
+        b_rbf_sb = held.tile([P, 1], F32, name="b_rbf_sb")
         nc.sync.dma_start(rbf_sb[:], rbf)
+        nc.sync.dma_start(b_rbf_sb[:], b_rbf)
         w_rbf_sb = held.tile([P, P], BF16, name="w_rbf_sb")
         nc.scalar.dma_start(w_rbf_sb[:], w_rbf)
-        b_rbf_sb = held.tile([P, 1], F32, name="b_rbf_sb")
-        nc.gpsimd.dma_start(b_rbf_sb[:], b_rbf)
 
         offsets = held.tile([P, EDGES // 16], U16, name="offsets")
         nc.sync.dma_start(offsets[:], offs)
@@ -34,11 +34,11 @@ def tile_embeddinglayer_kernel(
         h_dst_sb = held.tile([P, EDGES], BF16, name="h_dst_sb")
         nc.sync.dma_start(h_dst_sb[:], h_dst)
         w_dst_sb = held.tile([P, P], BF16, name="w_dst_sb")
-        nc.scalar.dma_start(w_dst_sb[:], w_rest[0:P, :])
+        nc.sync.dma_start(w_dst_sb[:], w_rest[0:P, :])
         w_p_sb = held.tile([P, P], BF16, name="w_p_sb")
         nc.scalar.dma_start(w_p_sb[:], w_rest[P : 2 * P, :])
         b_dense_sb = held.tile([P, 1], F32, name="b_dense_sb")
-        nc.gpsimd.dma_start(b_dense_sb[:], b_dense)
+        nc.sync.dma_start(b_dense_sb[:], b_dense)
 
         warm = held.tile([P, 1], F32, name="warm")
         nc.vector.memset(warm[:], 0.0)

@@ -33,12 +33,10 @@ def tile_embeddinglayer_kernel(
 
         h_dst_sb = held.tile([P, EDGES], BF16, name="h_dst_sb")
         nc.sync.dma_start(h_dst_sb[:], h_dst)
-        w_dst_sb = held.tile([P, P], BF16, name="w_dst_sb")
-        nc.sync.dma_start(w_dst_sb[:], w_rest[0:P, :])
-        w_p_sb = held.tile([P, P], BF16, name="w_p_sb")
-        nc.scalar.dma_start(w_p_sb[:], w_rest[P : 2 * P, :])
+        w_rest_sb = held.tile([P, 2, P], BF16, name="w_rest_sb")
+        nc.scalar.dma_start(w_rest_sb[:], w_rest.rearrange("(a k) m -> k a m", k=P))
         b_dense_sb = held.tile([P, 1], F32, name="b_dense_sb")
-        nc.sync.dma_start(b_dense_sb[:], b_dense)
+        nc.gpsimd.dma_start(b_dense_sb[:], b_dense)
 
         warm = held.tile([P, 1], F32, name="warm")
         nc.vector.memset(warm[:], 0.0)
@@ -53,8 +51,8 @@ def tile_embeddinglayer_kernel(
         nc.tensor.matmul(
             acc[:], w_src_sb[:], table_sb[:].indirect(offsets[:]), start=True, stop=False
         )
-        nc.tensor.matmul(acc[:], w_dst_sb[:], h_dst_sb[:], start=False, stop=False)
-        nc.tensor.matmul(acc[:], w_p_sb[:], p_sb[:], start=False, stop=True)
+        nc.tensor.matmul(acc[:], w_rest_sb[:, 0, :], h_dst_sb[:], start=False, stop=False)
+        nc.tensor.matmul(acc[:], w_rest_sb[:, 1, :], p_sb[:], start=False, stop=True)
 
         out_sb = held.tile([P, EDGES], F32, name="out_sb")
         nc.scalar.activation(out_sb[:], acc[:], SILU, bias=b_dense_sb[:])

@@ -18,14 +18,14 @@ def tile_embeddinglayer_kernel(
         tc.psum_pool(name="psum", bufs=1) as psum,
     ):
         rbf_sb = held.tile([P, EDGES], BF16, name="rbf_sb")
-        b_rbf_sb = held.tile([P, 1], F32, name="b_rbf_sb")
         nc.sync.dma_start(rbf_sb[:], rbf)
-        nc.sync.dma_start(b_rbf_sb[:], b_rbf)
         w_rbf_sb = held.tile([P, P], BF16, name="w_rbf_sb")
         nc.scalar.dma_start(w_rbf_sb[:], w_rbf)
 
         offsets = held.tile([P, EDGES // 16], U16, name="offsets")
         nc.sync.dma_start(offsets[:], offs)
+        b_rbf_sb = held.tile([P, 1], F32, name="b_rbf_sb")
+        nc.scalar.dma_start(b_rbf_sb[:], b_rbf)
         table_sb = held.tile([P, ATOMS], BF16, name="table_sb")
         nc.sync.dma_start(table_sb[:], table)
         w_src_sb = held.tile([P, P], BF16, name="w_src_sb")
@@ -34,7 +34,7 @@ def tile_embeddinglayer_kernel(
         h_dst_sb = held.tile([P, EDGES], BF16, name="h_dst_sb")
         nc.sync.dma_start(h_dst_sb[:], h_dst)
         w_rest_sb = held.tile([P, 2, P], BF16, name="w_rest_sb")
-        nc.scalar.dma_start(w_rest_sb[:], w_rest.rearrange("(a k) m -> k a m", k=P))
+        nc.sync.dma_start(w_rest_sb[:], w_rest.rearrange("(a k) m -> k a m", k=P))
         b_dense_sb = held.tile([P, 1], F32, name="b_dense_sb")
         nc.gpsimd.dma_start(b_dense_sb[:], b_dense)
 

@@ -31,10 +31,10 @@ def tile_embeddinglayer_kernel(
         w_src_sb = held.tile([P, P], BF16, name="w_src_sb")
         nc.scalar.dma_start(w_src_sb[:], w_src)
 
-        h_dst_sb = held.tile([P, EDGES], BF16, name="h_dst_sb")
-        nc.sync.dma_start(h_dst_sb[:], h_dst)
         w_rest_sb = held.tile([P, 2, P], BF16, name="w_rest_sb")
         nc.sync.dma_start(w_rest_sb[:], w_rest.rearrange("(a k) m -> k a m", k=P))
+        h_dst_sb = held.tile([P, EDGES], BF16, name="h_dst_sb")
+        nc.sync.dma_start(h_dst_sb[:], h_dst)
         b_dense_sb = held.tile([P, 1], F32, name="b_dense_sb")
         nc.gpsimd.dma_start(b_dense_sb[:], b_dense)
 

@@ -29,7 +29,7 @@ def tile_embeddinglayer_kernel(
         table_sb = held.tile([P, ATOMS], BF16, name="table_sb")
         nc.sync.dma_start(table_sb[:], table)
         w_src_sb = held.tile([P, P], BF16, name="w_src_sb")
-        nc.scalar.dma_start(w_src_sb[:], w_src)
+        nc.sync.dma_start(w_src_sb[:], w_src)
 
         w_rest_sb = held.tile([P, 2, P], BF16, name="w_rest_sb")
         nc.sync.dma_start(w_rest_sb[:], w_rest.rearrange("(a k) m -> k a m", k=P))

@@ -36,7 +36,7 @@ def tile_embeddinglayer_kernel(
         h_dst_sb = held.tile([P, EDGES], BF16, name="h_dst_sb")
         nc.sync.dma_start(h_dst_sb[:], h_dst)
         b_dense_sb = held.tile([P, 1], F32, name="b_dense_sb")
-        nc.gpsimd.dma_start(b_dense_sb[:], b_dense)
+        nc.sync.dma_start(b_dense_sb[:], b_dense)
 
         warm = held.tile([P, 1], F32, name="warm")
         nc.vector.memset(warm[:], 0.0)

@@ -3,6 +3,7 @@ import concourse.mybir as mybir
 P = 128
 ATOMS = 256
 EDGES = 128
+HALF = EDGES // 2
 FLOPS = 2 * 4 * P * P * EDGES
 
 BF16, F32, U16 = mybir.dt.bfloat16, mybir.dt.float32, mybir.dt.uint16
@@ -42,17 +43,25 @@ def tile_embeddinglayer_kernel(
         nc.vector.memset(warm[:], 0.0)
         nc.scalar.activation(warm[:], warm[:], SILU)
 
-        proj = psum.tile([P, EDGES], F32, name="proj")
-        nc.tensor.matmul(proj[:], w_rbf_sb[:], rbf_sb[:], start=True, stop=True)
-        p_sb = held.tile([P, EDGES], BF16, name="p_sb")
-        nc.scalar.activation(p_sb[:], proj[:], SILU, bias=b_rbf_sb[:])
+        halves = [slice(h * HALF, (h + 1) * HALF) for h in range(2)]
+        proj_halves = [psum.tile([P, HALF], F32, name=f"proj_half{h}") for h in range(2)]
+        p_halves = [held.tile([P, HALF], BF16, name=f"p_half{h}") for h in range(2)]
+        for h in range(2):
+            nc.tensor.matmul(
+                proj_halves[h][:], w_rbf_sb[:], rbf_sb[:, halves[h]], start=True, stop=True
+            )
+        for h in range(2):
+            nc.scalar.activation(p_halves[h][:], proj_halves[h][:], SILU, bias=b_rbf_sb[:])
 
         acc = psum.tile([P, EDGES], F32, name="acc")
         nc.tensor.matmul(
             acc[:], w_src_sb[:], table_sb[:].indirect(offsets[:]), start=True, stop=False
         )
         nc.tensor.matmul(acc[:], w_rest_sb[:, 0, :], h_dst_sb[:], start=False, stop=False)
-        nc.tensor.matmul(acc[:], w_rest_sb[:, 1, :], p_sb[:], start=False, stop=True)
+        for h in range(2):
+            nc.tensor.matmul(
+                acc[:, halves[h]], w_rest_sb[:, 1, :], p_halves[h][:], start=False, stop=(h == 1)
+            )
 
         out_sb = held.tile([P, EDGES], F32, name="out_sb")
         nc.scalar.activation(out_sb[:], acc[:], SILU, bias=b_dense_sb[:])

import concourse.mybir as mybir

P = 128
ATOMS = 256
EDGES = 128
HALF = EDGES // 2
FLOPS = 2 * 4 * P * P * EDGES

BF16, F32, U16 = mybir.dt.bfloat16, mybir.dt.float32, mybir.dt.uint16
SILU = mybir.ActivationFunctionType.Silu


def tile_embeddinglayer_kernel(
    tc, table, w_src, h_dst, rbf, w_rbf, b_rbf, w_rest, b_dense, offs, out
):
    nc = tc.nc
    with (
        tc.tile_pool(name="held", bufs=1) as held,
        tc.psum_pool(name="psum", bufs=1) as psum,
    ):
        rbf_sb = held.tile([P, EDGES], BF16, name="rbf_sb")
        nc.sync.dma_start(rbf_sb[:], rbf)
        w_rbf_sb = held.tile([P, P], BF16, name="w_rbf_sb")
        nc.scalar.dma_start(w_rbf_sb[:], w_rbf)

        offsets = held.tile([P, EDGES // 16], U16, name="offsets")
        nc.sync.dma_start(offsets[:], offs)
        b_rbf_sb = held.tile([P, 1], F32, name="b_rbf_sb")
        nc.scalar.dma_start(b_rbf_sb[:], b_rbf)
        table_sb = held.tile([P, ATOMS], BF16, name="table_sb")
        nc.sync.dma_start(table_sb[:], table)
        w_src_sb = held.tile([P, P], BF16, name="w_src_sb")
        nc.sync.dma_start(w_src_sb[:], w_src)

        w_rest_sb = held.tile([P, 2, P], BF16, name="w_rest_sb")
        nc.sync.dma_start(w_rest_sb[:], w_rest.rearrange("(a k) m -> k a m", k=P))
        h_dst_sb = held.tile([P, EDGES], BF16, name="h_dst_sb")
        nc.sync.dma_start(h_dst_sb[:], h_dst)
        b_dense_sb = held.tile([P, 1], F32, name="b_dense_sb")
        nc.sync.dma_start(b_dense_sb[:], b_dense)

        warm = held.tile([P, 1], F32, name="warm")
        nc.vector.memset(warm[:], 0.0)
        nc.scalar.activation(warm[:], warm[:], SILU)

        halves = [slice(h * HALF, (h + 1) * HALF) for h in range(2)]
        proj_halves = [psum.tile([P, HALF], F32, name=f"proj_half{h}") for h in range(2)]
        p_halves = [held.tile([P, HALF], BF16, name=f"p_half{h}") for h in range(2)]
        for h in range(2):
            nc.tensor.matmul(
                proj_halves[h][:], w_rbf_sb[:], rbf_sb[:, halves[h]], start=True, stop=True
            )
        for h in range(2):
            nc.scalar.activation(p_halves[h][:], proj_halves[h][:], SILU, bias=b_rbf_sb[:])

        acc = psum.tile([P, EDGES], F32, name="acc")
        nc.tensor.matmul(
            acc[:], w_src_sb[:], table_sb[:].indirect(offsets[:]), start=True, stop=False
        )
        nc.tensor.matmul(acc[:], w_rest_sb[:, 0, :], h_dst_sb[:], start=False, stop=False)
        for h in range(2):
            nc.tensor.matmul(
                acc[:, halves[h]], w_rest_sb[:, 1, :], p_halves[h][:], start=False, stop=(h == 1)
            )

        out_sb = held.tile([P, EDGES], F32, name="out_sb")
        nc.scalar.activation(out_sb[:], acc[:], SILU, bias=b_dense_sb[:])
        nc.sync.dma_start(out, out_sb[:])
